import numpy as np
import ml_dtypes


def mxq(x, axis, fmt="e4m3"):
    dtype, down = {"e4m3": (ml_dtypes.float8_e4m3fn, 7), "e5m2": (ml_dtypes.float8_e5m2, 14)}[fmt]
    v = np.moveaxis(np.asarray(x, np.float32).astype(ml_dtypes.bfloat16).astype(np.float64), axis, -1)
    blocks = v.reshape(v.shape[:-1] + (-1, 32))
    amax = np.abs(blocks).max(-1, keepdims=True)
    byte = np.maximum(np.where(amax > 0, np.frexp(amax)[1] - 1 + 127, 0) - down, 1)
    scale = np.exp2(byte - 127.0)
    codes = (blocks / scale).astype(np.float32).astype(dtype).astype(np.float64)
    return np.moveaxis((codes * scale).reshape(v.shape), -1, axis)


WIDE = False


def mx_kscale(k):
    if not WIDE:
        return np.ones(k)
    levels = np.array([10, -10, 5, -5, 0])
    if k % 512:
        return np.exp2(np.random.permutation(np.resize(levels, k // 32))).repeat(32)
    a = np.empty((k // 512, 16))
    for p in range(k // 512):
        a[p, :8] = np.random.permutation(np.resize(levels, 8))
        for g in range(8):
            far = levels[np.abs(levels - a[p, g]) >= 10]
            a[p, g + 8] = far[np.random.randint(len(far))]
    return np.exp2(a.ravel()).repeat(32)


BF16 = ml_dtypes.bfloat16


def bf(x):
    return np.asarray(x, np.float32).astype(BF16)


def f64(x):
    return np.asarray(x).astype(np.float64)


T, D, F, R = 512, 1024, 2560, 128


def setup_inputs():
    s = mx_kscale(F)
    return {
        "h": bf(np.random.standard_normal((T, F)) * 0.75 * s),
        "ha": bf(np.random.standard_normal((T, R)) * 0.75),
        "W_down": bf(np.random.standard_normal((F, D)) / np.sqrt(F) / s[:, None]),
        "B_down": bf(np.random.standard_normal((R, D)) * 0.5 / np.sqrt(R)),
    }


def reference(h, ha, W_down, B_down):
    return (mxq(f64(h), 1, "e4m3") @ mxq(f64(W_down), 0, "e4m3")) + f64(ha) @ f64(B_down)

@@ -1,0 +1,210 @@
+from contextlib import ExitStack
+
+import concourse.mybir as mybir
+from concourse.masks import make_identity
+
+F32 = mybir.dt.float32
+BF16 = mybir.dt.bfloat16
+U32 = mybir.dt.uint32
+U8 = mybir.dt.uint8
+FP8X4 = mybir.dt.float8_e4m3fn_x4
+ADD = mybir.AluOpType.add
+
+P = 128
+T, D, F, R = 512, 1024, 2560, 128
+K_PASS = 512
+G = F // K_PASS
+NT = T // P
+NC = D // 512
+
+FLOPS = 2 * T * F * D + 2 * T * R * D
+
+DMA_ORDER = ["ha","B","W0","h0","h1","h2","h3","W1","W2","W3","W4"]
+SPLIT_CHUNKS = []
+VCOLS = [[512,512],[256,256],[256,256],[256,256],[224,256]]
+LORA_ENG = ["V","S","V","S","V","S","V","S"]
+H_ENG = []
+W_ORDER = [[0,0],[0,1],[1,0],[1,1],[2,0],[2,1],[3,0],[3,1],[4,0],[4,1]]
+MANUAL = True
+PROGRAM = [["LH"],["L",0,0],["L",1,0],["L",2,0],["L",3,0],["L",0,1],["L",1,1],["L",2,1],["L",3,1],["WR",0,0],["WR",0,1],["WQ",0,0],["WQ",0,1],["HB",0,0,"S"],["HB",0,2,"S"],["HB",1,0,"S"],["HB",1,2,"S"],["HL",0,"S"],["HQ",0],["HQ",1],["HB",2,0,"S"],["HB",2,2,"S"],["HB",3,0,"S"],["HB",3,2,"S"],["HL",2,"S"],["HQ",2],["HQ",3],["HQL"],["P",0,0,0],["P",0,0,1],["P",0,0,2],["P",0,0,3],["P",0,1,0],["P",0,1,1],["P",0,1,2],["P",0,1,3],["WR",1,0],["WR",1,1],["WQ",1,0],["P",1,0,0],["P",1,0,1],["P",1,0,2],["P",1,0,3],["WQ",1,1],["P",1,1,0],["P",1,1,1],["P",1,1,2],["P",1,1,3],["WR",2,0],["WR",2,1],["WQ",2,0],["P",2,0,0],["P",2,0,1],["P",2,0,2],["P",2,0,3],["WQ",2,1],["P",2,1,0],["P",2,1,1],["P",2,1,2],["P",2,1,3],["WR",3,0],["WR",3,1],["WQ",3,0],["P",3,0,0],["P",3,0,1],["P",3,0,2],["P",3,0,3],["WQ",3,1],["P",3,1,0],["P",3,1,1],["P",3,1,2],["P",3,1,3],["WR",4,0],["WR",4,1],["WQ",4,0],["P",4,0,0],["P",4,0,1],["P",4,0,2],["P",4,0,3],["WQ",4,1],["P",4,1,0],["P",4,1,1],["P",4,1,2],["P",4,1,3],["F",0,0],["F",1,0],["F",2,0],["F",3,0],["F",0,1],["F",1,1],["F",2,1],["F",3,1]]
+
+
+def tile_loramlp_pb_kernel(tc, h, ha, W_down, B_down, out):
+    nc = tc.nc
+    with ExitStack() as ctx:
+        keep = ctx.enter_context(tc.tile_pool(name="keep", bufs=1))
+        psum = ctx.enter_context(tc.psum_pool(name="psum", bufs=8))
+        if MANUAL:
+            ctx.enter_context(tc.manual_schedule())
+
+        h_v = h.rearrange("(p i) k -> p i k", i=NT)
+        out_v = out.rearrange("(p i) d -> p i d", i=NT)
+
+        ha_sb = keep.tile([P, NT, R], BF16, name="ha_sb")
+        b_sb = keep.tile([P, D], BF16, name="b_sb")
+        h_raw = [keep.tile([P, F], BF16, name="h_raw%d" % i) for i in range(NT)]
+        w_raw = {}
+        for g in range(G):
+            if g in SPLIT_CHUNKS:
+                for c in range(NC):
+                    w_raw[(g, c)] = keep.tile([P, 4, 512], BF16, name="w_raw%d%d" % (g, c))
+            else:
+                w_raw[(g, 0)] = keep.tile([P, 4, D], BF16, name="w_raw%d" % g)
+
+        for what in DMA_ORDER:
+            if what == "ha":
+                nc.sync.dma_start(out=ha_sb[:], in_=ha.rearrange("(p i) r -> p i r", i=NT))
+            elif what == "B":
+                nc.sync.dma_start(out=b_sb[:], in_=B_down)
+            elif what[0] == "h":
+                i = int(what[1])
+                nc.sync.dma_start(out=h_raw[i][:], in_=h_v[:, i, :])
+            elif len(what) == 2:
+                g = int(what[1])
+                nc.sync.dma_start(
+                    out=w_raw[(g, 0)][:].rearrange("p e c -> p (e c)"),
+                    in_=W_down[g * K_PASS : (g + 1) * K_PASS, :].rearrange("(p e) c -> p (e c)", e=4),
+                )
+            else:
+                g = int(what[1])
+                c = 0 if what[2] == "a" else 1
+                nc.sync.dma_start(
+                    out=w_raw[(g, c)][:],
+                    in_=W_down[g * K_PASS : (g + 1) * K_PASS, c * 512 : (c + 1) * 512].rearrange("(p e) c -> p e c", e=4),
+                )
+
+        ident_b = keep.tile([P, P], BF16, name="ident_b")
+        make_identity(nc, ident_b[:])
+        ident_f = keep.tile([P, P], F32, name="ident_f")
+        make_identity(nc, ident_f[:])
+
+        def evacuate(eng, dst, src):
+            if eng == "S":
+                nc.scalar.copy(out=dst, in_=src)
+            else:
+                nc.vector.tensor_copy(out=dst, in_=src)
+
+        lora = [keep.tile([P, D], F32, name="lora%d" % i) for i in range(NT)]
+        haT = keep.tile([P, NT, P], BF16, name="haT")
+
+        def lora_head():
+            haT_ps = psum.tile([P, NT, P], BF16, name="haT_ps", tag="bank")
+            for i in range(NT):
+                nc.tensor.transpose(haT_ps[:, i, :], ha_sb[:, i, :], ident_b[:])
+            nc.vector.tensor_copy(out=haT[:], in_=haT_ps[:])
+
+        def lora_mm(i, c):
+            ps = psum.tile([P, 512], F32, name="lora_ps", tag="bank")
+            nc.tensor.matmul(out=ps[:], lhsT=haT[:, i, :], rhs=b_sb[:, c * 512 : (c + 1) * 512], start=True, stop=True)
+            evacuate(LORA_ENG[c * NT + i], lora[i][:, c * 512 : (c + 1) * 512], ps[:])
+
+        hg_a = [keep.tile([P, 2048], BF16, name="hg_a%d" % i, align_bytes=64) for i in range(NT)]
+        hc_a = [keep.tile([P, 512], U32, name="hc_a%d" % i, align_bytes=64) for i in range(NT)]
+        hs_a = [keep.tile([P, 512], U8, name="hs_a%d" % i, align_bytes=64) for i in range(NT)]
+        hg_b = keep.tile([P, 2048], BF16, name="hg_b", align_bytes=64)
+        hc_b = keep.tile([P, 512], U32, name="hc_b", align_bytes=64)
+        hs_b = keep.tile([P, 512], U8, name="hs_b", align_bytes=64)
+
+        def words(i, g, u):
+            return h_raw[i][:].bitcast(F32)[:, 256 * g + u : 256 * (g + 1) : 2]
+
+        def h_bank(i, g0, eng):
+            dst32 = hg_a[i][:].bitcast(F32).rearrange("p (g r u) -> p g r u", g=4, r=P, u=2)
+            xt = psum.tile([P, 2, 2, P], F32, name="xt", tag="bank")
+            for gg in range(2):
+                for u in range(2):
+                    nc.tensor.transpose(xt[:, gg, u, :], words(i, g0 + gg, u), ident_f[:])
+            evacuate(eng, dst32[:, g0 : g0 + 2], xt[:].rearrange("p g u r -> p g r u"))
+
+        def h_last(i0, eng):
+            dst32 = hg_b[:].bitcast(F32).rearrange("p (i r u) -> p i r u", i=NT, r=P, u=2)
+            xt = psum.tile([P, 2, 2, P], F32, name="xt", tag="bank")
+            for ii in range(2):
+                for u in range(2):
+                    nc.tensor.transpose(xt[:, ii, u, :], words(i0 + ii, 4, u), ident_f[:])
+            evacuate(eng, dst32[:, i0 : i0 + 2], xt[:].rearrange("p g u r -> p g r u"))
+
+        def h_quant(i):
+            nc.vector.quantize_mx(out=hc_a[i][:].bitcast(FP8X4), scales=hs_a[i][:], in_=hg_a[i][:])
+
+        def h_quant_last():
+            nc.vector.quantize_mx(out=hc_b[:].bitcast(FP8X4), scales=hs_b[:], in_=hg_b[:])
+
+        wg = {}
+        wc = {}
+        ws = {}
+
+        def w_regroup(g, c):
+            wg[(g, c)] = keep.tile([P, 512, 4], BF16, name="wg%d%d" % (g, c), align_bytes=64)
+            if g in SPLIT_CHUNKS:
+                src = w_raw[(g, c)][:]
+            else:
+                src = w_raw[(g, 0)][:, :, c * 512 : (c + 1) * 512]
+            a = VCOLS[g][c]
+            if a > 0:
+                nc.vector.tensor_copy(
+                    out=wg[(g, c)][:, 0:a, :].rearrange("p (c i) t -> p c t i", i=4),
+                    in_=src[:, :, 0:a].rearrange("p t (c i) -> p c t i", i=4),
+                )
+            if a < 512:
+                nc.scalar.copy(
+                    out=wg[(g, c)][:, a:512, :].rearrange("p (c i) t -> p c t i", i=4),
+                    in_=src[:, :, a:512].rearrange("p t (c i) -> p c t i", i=4),
+                )
+
+        def w_quant(g, c):
+            wc[(g, c)] = keep.tile([P, 512], U32, name="wc%d%d" % (g, c), align_bytes=64)
+            ws[(g, c)] = keep.tile([P, 512], U8, name="ws%d%d" % (g, c), align_bytes=64)
+            nc.vector.quantize_mx(
+                out=wc[(g, c)][:].bitcast(FP8X4), scales=ws[(g, c)][:], in_=wg[(g, c)][:].rearrange("p c t -> p (c t)")
+            )
+
+        acc = {}
+        done = {}
+
+        def mx_pass(g, c, i):
+            if (i, c) not in acc:
+                acc[(i, c)] = psum.tile([P, 512], F32, name="acc%d%d" % (i, c), tag="bank")
+                done[(i, c)] = 0
+            if g < 4:
+                lhsT, lsc = hc_a[i][:, g * P : (g + 1) * P], hs_a[i][:, g * P : (g + 1) * P]
+            else:
+                lhsT, lsc = hc_b[:, i * P : (i + 1) * P], hs_b[:, i * P : (i + 1) * P]
+            nc.tensor.matmul_mx(
+                out=acc[(i, c)][:],
+                lhsT=lhsT.bitcast(FP8X4),
+                lhsT_scale=lsc,
+                rhs=wc[(g, c)][:].bitcast(FP8X4),
+                rhs_scale=ws[(g, c)][:],
+                start=(done[(i, c)] == 0),
+                stop=(done[(i, c)] == G - 1),
+            )
+            done[(i, c)] += 1
+
+        def finish(i, c):
+            cs = slice(c * 512, (c + 1) * 512)
+            nc.vector.tensor_tensor(out=lora[i][:, cs], in0=acc[(i, c)][:], in1=lora[i][:, cs], op=ADD)
+            nc.sync.dma_start(out=out_v[:, i, cs], in_=lora[i][:, cs])
+
+        for step in PROGRAM:
+            op = step[0]
+            if op == "LH":
+                lora_head()
+            elif op == "L":
+                lora_mm(step[1], step[2])
+            elif op == "HB":
+                h_bank(step[1], step[2], step[3])
+            elif op == "HL":
+                h_last(step[1], step[2])
+            elif op == "HQ":
+                h_quant(step[1])
+            elif op == "HQL":
+                h_quant_last()
+            elif op == "WR":
+                w_regroup(step[1], step[2])
+            elif op == "WQ":
+                w_quant(step[1], step[2])
+            elif op == "P":
+                mx_pass(step[1], step[2], step[3])
+            elif op == "F":
+                finish(step[1], step[2])

@@ -15,18 +15,17 @@ T, D, F, R = 512, 1024, 2560, 128
 K_PASS = 512
 G = F // K_PASS
 NT = T // P
-NC = D // 512
+HALF = 512
+LAST = G - 1
 
 FLOPS = 2 * T * F * D + 2 * T * R * D
 
-DMA_ORDER = ["ha","B","W0","h0","h1","h2","h3","W1","W2","W3","W4"]
-SPLIT_CHUNKS = []
-VCOLS = [[512,512],[256,256],[256,256],[256,256],[224,256]]
-LORA_ENG = ["V","S","V","S","V","S","V","S"]
-H_ENG = []
-W_ORDER = [[0,0],[0,1],[1,0],[1,1],[2,0],[2,1],[3,0],[3,1],[4,0],[4,1]]
-MANUAL = True
-PROGRAM = [["LH"],["L",0,0],["L",1,0],["L",2,0],["L",3,0],["L",0,1],["L",1,1],["L",2,1],["L",3,1],["WR",0,0],["WR",0,1],["WQ",0,0],["WQ",0,1],["HB",0,0,"S"],["HB",0,2,"S"],["HB",1,0,"S"],["HB",1,2,"S"],["HL",0,"S"],["HQ",0],["HQ",1],["HB",2,0,"S"],["HB",2,2,"S"],["HB",3,0,"S"],["HB",3,2,"S"],["HL",2,"S"],["HQ",2],["HQ",3],["HQL"],["P",0,0,0],["P",0,0,1],["P",0,0,2],["P",0,0,3],["P",0,1,0],["P",0,1,1],["P",0,1,2],["P",0,1,3],["WR",1,0],["WR",1,1],["WQ",1,0],["P",1,0,0],["P",1,0,1],["P",1,0,2],["P",1,0,3],["WQ",1,1],["P",1,1,0],["P",1,1,1],["P",1,1,2],["P",1,1,3],["WR",2,0],["WR",2,1],["WQ",2,0],["P",2,0,0],["P",2,0,1],["P",2,0,2],["P",2,0,3],["WQ",2,1],["P",2,1,0],["P",2,1,1],["P",2,1,2],["P",2,1,3],["WR",3,0],["WR",3,1],["WQ",3,0],["P",3,0,0],["P",3,0,1],["P",3,0,2],["P",3,0,3],["WQ",3,1],["P",3,1,0],["P",3,1,1],["P",3,1,2],["P",3,1,3],["WR",4,0],["WR",4,1],["WQ",4,0],["P",4,0,0],["P",4,0,1],["P",4,0,2],["P",4,0,3],["WQ",4,1],["P",4,1,0],["P",4,1,1],["P",4,1,2],["P",4,1,3],["F",0,0],["F",1,0],["F",2,0],["F",3,0],["F",0,1],["F",1,1],["F",2,1],["F",3,1]]
+
+HALVES = [(1, 0), (1, 1), (2, 0), (3, 0), (4, 0), (2, 1), (3, 1), (4, 1)]
+
+
+def vector_columns(g, c):
+    return HALF if g == 0 else HALF // 2
 
 
 def tile_loramlp_pb_kernel(tc, h, ha, W_down, B_down, out):
@@ -34,44 +33,42 @@ def tile_loramlp_pb_kernel(tc, h, ha, W_down, B_down, out):
     with ExitStack() as ctx:
         keep = ctx.enter_context(tc.tile_pool(name="keep", bufs=1))
         psum = ctx.enter_context(tc.psum_pool(name="psum", bufs=8))
-        if MANUAL:
-            ctx.enter_context(tc.manual_schedule())
+        ctx.enter_context(tc.manual_schedule())
 
         h_v = h.rearrange("(p i) k -> p i k", i=NT)
         out_v = out.rearrange("(p i) d -> p i d", i=NT)
 
         ha_sb = keep.tile([P, NT, R], BF16, name="ha_sb")
         b_sb = keep.tile([P, D], BF16, name="b_sb")
-        h_raw = [keep.tile([P, F], BF16, name="h_raw%d" % i) for i in range(NT)]
-        w_raw = {}
-        for g in range(G):
-            if g in SPLIT_CHUNKS:
-                for c in range(NC):
-                    w_raw[(g, c)] = keep.tile([P, 4, 512], BF16, name="w_raw%d%d" % (g, c))
-            else:
-                w_raw[(g, 0)] = keep.tile([P, 4, D], BF16, name="w_raw%d" % g)
+        nc.sync.dma_start(out=ha_sb[:], in_=ha.rearrange("(p i) r -> p i r", i=NT))
+        nc.sync.dma_start(out=b_sb[:], in_=B_down)
+        w_half = {}
 
-        for what in DMA_ORDER:
-            if what == "ha":
-                nc.sync.dma_start(out=ha_sb[:], in_=ha.rearrange("(p i) r -> p i r", i=NT))
-            elif what == "B":
-                nc.sync.dma_start(out=b_sb[:], in_=B_down)
-            elif what[0] == "h":
-                i = int(what[1])
-                nc.sync.dma_start(out=h_raw[i][:], in_=h_v[:, i, :])
-            elif len(what) == 2:
-                g = int(what[1])
-                nc.sync.dma_start(
-                    out=w_raw[(g, 0)][:].rearrange("p e c -> p (e c)"),
-                    in_=W_down[g * K_PASS : (g + 1) * K_PASS, :].rearrange("(p e) c -> p (e c)", e=4),
-                )
-            else:
-                g = int(what[1])
-                c = 0 if what[2] == "a" else 1
-                nc.sync.dma_start(
-                    out=w_raw[(g, c)][:],
-                    in_=W_down[g * K_PASS : (g + 1) * K_PASS, c * 512 : (c + 1) * 512].rearrange("(p e) c -> p e c", e=4),
-                )
+        def load_half(g, c):
+            wh = keep.tile([P, 4, HALF], BF16, name="w_raw%d%d" % (g, c))
+            nc.sync.dma_start(
+                out=wh[:],
+                in_=W_down[g * K_PASS : (g + 1) * K_PASS, c * HALF : (c + 1) * HALF].rearrange("(p t) c -> p t c", t=4),
+            )
+            w_half[(g, c)] = wh[:]
+
+        load_half(0, 0)
+        load_half(0, 1)
+        h_raw = []
+        for i in range(NT):
+            h_raw.append(keep.tile([P, F], BF16, name="h_raw%d" % i))
+            nc.sync.dma_start(out=h_raw[i][:], in_=h_v[:, i, :])
+        for g in (1, 2):
+            wg = keep.tile([P, 4, D], BF16, name="w_raw%d" % g)
+            nc.sync.dma_start(
+                out=wg[:].rearrange("p t c -> p (t c)"),
+                in_=W_down[g * K_PASS : (g + 1) * K_PASS, :].rearrange("(p t) c -> p (t c)", t=4),
+            )
+            for c in range(2):
+                w_half[(g, c)] = wg[:, :, c * HALF : (c + 1) * HALF]
+        for c in range(2):
+            for g in (3, 4):
+                load_half(g, c)
 
         ident_b = keep.tile([P, P], BF16, name="ident_b")
         make_identity(nc, ident_b[:])
@@ -86,125 +83,111 @@ def tile_loramlp_pb_kernel(tc, h, ha, W_down, B_down, out):
 
         lora = [keep.tile([P, D], F32, name="lora%d" % i) for i in range(NT)]
         haT = keep.tile([P, NT, P], BF16, name="haT")
-
-        def lora_head():
-            haT_ps = psum.tile([P, NT, P], BF16, name="haT_ps", tag="bank")
+        haT_ps = psum.tile([P, NT, P], BF16, name="haT_ps", tag="bank")
+        for i in range(NT):
+            nc.tensor.transpose(haT_ps[:, i, :], ha_sb[:, i, :], ident_b[:])
+        nc.scalar.copy(out=haT[:], in_=haT_ps[:])
+        for c in range(2):
             for i in range(NT):
-                nc.tensor.transpose(haT_ps[:, i, :], ha_sb[:, i, :], ident_b[:])
-            nc.vector.tensor_copy(out=haT[:], in_=haT_ps[:])
+                cs = slice(c * HALF, (c + 1) * HALF)
+                ps = psum.tile([P, HALF], F32, name="lora_ps", tag="bank")
+                nc.tensor.matmul(out=ps[:], lhsT=haT[:, i, :], rhs=b_sb[:, cs], start=True, stop=True)
+                nc.scalar.copy(out=lora[i][:, cs], in_=ps[:])
 
-        def lora_mm(i, c):
-            ps = psum.tile([P, 512], F32, name="lora_ps", tag="bank")
-            nc.tensor.matmul(out=ps[:], lhsT=haT[:, i, :], rhs=b_sb[:, c * 512 : (c + 1) * 512], start=True, stop=True)
-            evacuate(LORA_ENG[c * NT + i], lora[i][:, c * 512 : (c + 1) * 512], ps[:])
-
-        hg_a = [keep.tile([P, 2048], BF16, name="hg_a%d" % i, align_bytes=64) for i in range(NT)]
-        hc_a = [keep.tile([P, 512], U32, name="hc_a%d" % i, align_bytes=64) for i in range(NT)]
-        hs_a = [keep.tile([P, 512], U8, name="hs_a%d" % i, align_bytes=64) for i in range(NT)]
-        hg_b = keep.tile([P, 2048], BF16, name="hg_b", align_bytes=64)
-        hc_b = keep.tile([P, 512], U32, name="hc_b", align_bytes=64)
-        hs_b = keep.tile([P, 512], U8, name="hs_b", align_bytes=64)
-
-        def words(i, g, u):
-            return h_raw[i][:].bitcast(F32)[:, 256 * g + u : 256 * (g + 1) : 2]
-
-        def h_bank(i, g0, eng):
-            dst32 = hg_a[i][:].bitcast(F32).rearrange("p (g r u) -> p g r u", g=4, r=P, u=2)
-            xt = psum.tile([P, 2, 2, P], F32, name="xt", tag="bank")
-            for gg in range(2):
-                for u in range(2):
-                    nc.tensor.transpose(xt[:, gg, u, :], words(i, g0 + gg, u), ident_f[:])
-            evacuate(eng, dst32[:, g0 : g0 + 2], xt[:].rearrange("p g u r -> p g r u"))
-
-        def h_last(i0, eng):
-            dst32 = hg_b[:].bitcast(F32).rearrange("p (i r u) -> p i r u", i=NT, r=P, u=2)
-            xt = psum.tile([P, 2, 2, P], F32, name="xt", tag="bank")
-            for ii in range(2):
-                for u in range(2):
-                    nc.tensor.transpose(xt[:, ii, u, :], words(i0 + ii, 4, u), ident_f[:])
-            evacuate(eng, dst32[:, i0 : i0 + 2], xt[:].rearrange("p g u r -> p g r u"))
-
-        def h_quant(i):
-            nc.vector.quantize_mx(out=hc_a[i][:].bitcast(FP8X4), scales=hs_a[i][:], in_=hg_a[i][:])
-
-        def h_quant_last():
-            nc.vector.quantize_mx(out=hc_b[:].bitcast(FP8X4), scales=hs_b[:], in_=hg_b[:])
-
-        wg = {}
+        wg4 = {}
         wc = {}
         ws = {}
 
         def w_regroup(g, c):
-            wg[(g, c)] = keep.tile([P, 512, 4], BF16, name="wg%d%d" % (g, c), align_bytes=64)
-            if g in SPLIT_CHUNKS:
-                src = w_raw[(g, c)][:]
-            else:
-                src = w_raw[(g, 0)][:, :, c * 512 : (c + 1) * 512]
-            a = VCOLS[g][c]
-            if a > 0:
-                nc.vector.tensor_copy(
-                    out=wg[(g, c)][:, 0:a, :].rearrange("p (c i) t -> p c t i", i=4),
-                    in_=src[:, :, 0:a].rearrange("p t (c i) -> p c t i", i=4),
-                )
-            if a < 512:
-                nc.scalar.copy(
-                    out=wg[(g, c)][:, a:512, :].rearrange("p (c i) t -> p c t i", i=4),
-                    in_=src[:, :, a:512].rearrange("p t (c i) -> p c t i", i=4),
-                )
+            wg4[(g, c)] = keep.tile([P, HALF, 4], BF16, name="wg%d%d" % (g, c), align_bytes=64)
+            a = vector_columns(g, c)
+            for eng, lo, hi in (("S", a, HALF), ("V", 0, a)):
+                if lo < hi:
+                    evacuate(
+                        eng,
+                        wg4[(g, c)][:, lo:hi, :].rearrange("p (c i) t -> p c t i", i=4),
+                        w_half[(g, c)][:, :, lo:hi].rearrange("p t (c i) -> p c t i", i=4),
+                    )
 
         def w_quant(g, c):
-            wc[(g, c)] = keep.tile([P, 512], U32, name="wc%d%d" % (g, c), align_bytes=64)
-            ws[(g, c)] = keep.tile([P, 512], U8, name="ws%d%d" % (g, c), align_bytes=64)
+            wc[(g, c)] = keep.tile([P, HALF], U32, name="wc%d%d" % (g, c), align_bytes=64)
+            ws[(g, c)] = keep.tile([P, HALF], U8, name="ws%d%d" % (g, c), align_bytes=64)
             nc.vector.quantize_mx(
-                out=wc[(g, c)][:].bitcast(FP8X4), scales=ws[(g, c)][:], in_=wg[(g, c)][:].rearrange("p c t -> p (c t)")
+                out=wc[(g, c)][:].bitcast(FP8X4), scales=ws[(g, c)][:], in_=wg4[(g, c)][:].rearrange("p c t -> p (c t)")
             )
+
+        for c in range(2):
+            w_regroup(0, c)
+        for c in range(2):
+            w_quant(0, c)
+
+        hg = [keep.tile([P, 2048], BF16, name="hg%d" % i, align_bytes=64) for i in range(NT + 1)]
+        hc = [keep.tile([P, 512], U32, name="hc%d" % i, align_bytes=64) for i in range(NT + 1)]
+        hs = [keep.tile([P, 512], U8, name="hs%d" % i, align_bytes=64) for i in range(NT + 1)]
+
+        def h_bank(which, b, blocks, eng):
+            dst = hg[which][:].bitcast(F32).rearrange("p (b r u) -> p b r u", b=4, r=P, u=2)
+            xt = psum.tile([P, 2, 2, P], F32, name="xt", tag="bank")
+            for n, (i, g) in enumerate(blocks):
+                words = h_raw[i][:].bitcast(F32)
+                for u in range(2):
+                    nc.tensor.transpose(xt[:, n, u, :], words[:, 256 * g + u : 256 * (g + 1) : 2], ident_f[:])
+            evacuate(eng, dst[:, b : b + 2], xt[:].rearrange("p b u r -> p b r u"))
+
+        def h_quant(which):
+            nc.vector.quantize_mx(out=hc[which][:].bitcast(FP8X4), scales=hs[which][:], in_=hg[which][:])
+
+        for i in (0, 2):
+            h_bank(i, 0, [(i, 0), (i, 1)], "V")
+            h_bank(i, 2, [(i, 2), (i, 3)], "S")
+            h_bank(i + 1, 0, [(i + 1, 0), (i + 1, 1)], "V")
+            h_quant(i)
+            h_bank(i + 1, 2, [(i + 1, 2), (i + 1, 3)], "S")
+            h_bank(NT, i, [(i, LAST), (i + 1, LAST)], "S")
+            h_quant(i + 1)
+        h_quant(NT)
 
         acc = {}
-        done = {}
 
-        def mx_pass(g, c, i):
-            if (i, c) not in acc:
-                acc[(i, c)] = psum.tile([P, 512], F32, name="acc%d%d" % (i, c), tag="bank")
-                done[(i, c)] = 0
-            if g < 4:
-                lhsT, lsc = hc_a[i][:, g * P : (g + 1) * P], hs_a[i][:, g * P : (g + 1) * P]
+        def mx_passes(g, c):
+            for i in range(NT):
+                if g == 0:
+                    acc[(i, c)] = psum.tile([P, HALF], F32, name="acc%d%d" % (i, c), tag="bank")
+                which, block = (i, g) if g < LAST else (NT, i)
+                hw = slice(block * P, (block + 1) * P)
+                nc.tensor.matmul_mx(
+                    out=acc[(i, c)][:],
+                    lhsT=hc[which][:, hw].bitcast(FP8X4),
+                    lhsT_scale=hs[which][:, hw],
+                    rhs=wc[(g, c)][:].bitcast(FP8X4),
+                    rhs_scale=ws[(g, c)][:],
+                    start=(g == 0),
+                    stop=(g == LAST),
+                )
+
+        def finish(i, c, by_gpsimd=False):
+            cs = slice(c * HALF, (c + 1) * HALF)
+            if by_gpsimd:
+                sums = keep.tile([P, HALF], F32, name="sums%d%d" % (i, c))
+                nc.scalar.copy(out=sums[:], in_=acc[(i, c)][:])
+                nc.gpsimd.tensor_tensor(out=lora[i][:, cs], in0=sums[:], in1=lora[i][:, cs], op=ADD)
             else:
-                lhsT, lsc = hc_b[:, i * P : (i + 1) * P], hs_b[:, i * P : (i + 1) * P]
-            nc.tensor.matmul_mx(
-                out=acc[(i, c)][:],
-                lhsT=lhsT.bitcast(FP8X4),
-                lhsT_scale=lsc,
-                rhs=wc[(g, c)][:].bitcast(FP8X4),
-                rhs_scale=ws[(g, c)][:],
-                start=(done[(i, c)] == 0),
-                stop=(done[(i, c)] == G - 1),
-            )
-            done[(i, c)] += 1
-
-        def finish(i, c):
-            cs = slice(c * 512, (c + 1) * 512)
-            nc.vector.tensor_tensor(out=lora[i][:, cs], in0=acc[(i, c)][:], in1=lora[i][:, cs], op=ADD)
+                nc.vector.tensor_tensor(out=lora[i][:, cs], in0=acc[(i, c)][:], in1=lora[i][:, cs], op=ADD)
             nc.sync.dma_start(out=out_v[:, i, cs], in_=lora[i][:, cs])
 
-        for step in PROGRAM:
-            op = step[0]
-            if op == "LH":
-                lora_head()
-            elif op == "L":
-                lora_mm(step[1], step[2])
-            elif op == "HB":
-                h_bank(step[1], step[2], step[3])
-            elif op == "HL":
-                h_last(step[1], step[2])
-            elif op == "HQ":
-                h_quant(step[1])
-            elif op == "HQL":
-                h_quant_last()
-            elif op == "WR":
-                w_regroup(step[1], step[2])
-            elif op == "WQ":
-                w_quant(step[1], step[2])
-            elif op == "P":
-                mx_pass(step[1], step[2], step[3])
-            elif op == "F":
-                finish(step[1], step[2])
+        mx_passes(0, 0)
+        mx_passes(0, 1)
+        for n, (g, c) in enumerate(HALVES):
+            w_regroup(g, c)
+            if n > 0:
+                w_quant(*HALVES[n - 1])
+                mx_passes(*HALVES[n - 1])
+            if (g, c) == (3, 1):
+                finish(0, 0)
+                finish(1, 0, by_gpsimd=True)
+        finish(2, 0)
+        w_quant(LAST, 1)
+        mx_passes(LAST, 1)
+        finish(3, 0)
+        for i in range(NT):
+            finish(i, 1)

@@ -25,7 +25,11 @@ HALVES = [(1, 0), (1, 1), (2, 0), (3, 0), (4, 0), (2, 1), (3, 1), (4, 1)]
 
 
 def vector_columns(g, c):
-    return HALF if g == 0 else HALF // 2
+    if g == 0:
+        return HALF
+    if (g, c) == (LAST, 0):
+        return 384
+    return 128 if g > 1 and c == 1 else 256
 
 
 def tile_loramlp_pb_kernel(tc, h, ha, W_down, B_down, out):
@@ -52,13 +56,7 @@ def tile_loramlp_pb_kernel(tc, h, ha, W_down, B_down, out):
             )
             w_half[(g, c)] = wh[:]
 
-        load_half(0, 0)
-        load_half(0, 1)
-        h_raw = []
-        for i in range(NT):
-            h_raw.append(keep.tile([P, F], BF16, name="h_raw%d" % i))
-            nc.sync.dma_start(out=h_raw[i][:], in_=h_v[:, i, :])
-        for g in (1, 2):
+        def load_chunk(g):
             wg = keep.tile([P, 4, D], BF16, name="w_raw%d" % g)
             nc.sync.dma_start(
                 out=wg[:].rearrange("p t c -> p (t c)"),
@@ -66,6 +64,14 @@ def tile_loramlp_pb_kernel(tc, h, ha, W_down, B_down, out):
             )
             for c in range(2):
                 w_half[(g, c)] = wg[:, :, c * HALF : (c + 1) * HALF]
+
+        h_raw = []
+        load_chunk(0)
+        for i in range(NT):
+            h_raw.append(keep.tile([P, F], BF16, name="h_raw%d" % i))
+            nc.sync.dma_start(out=h_raw[i][:], in_=h_v[:, i, :])
+        load_chunk(1)
+        load_chunk(2)
         for c in range(2):
             for g in (3, 4):
                 load_half(g, c)
@@ -86,13 +92,13 @@ def tile_loramlp_pb_kernel(tc, h, ha, W_down, B_down, out):
         haT_ps = psum.tile([P, NT, P], BF16, name="haT_ps", tag="bank")
         for i in range(NT):
             nc.tensor.transpose(haT_ps[:, i, :], ha_sb[:, i, :], ident_b[:])
-        nc.scalar.copy(out=haT[:], in_=haT_ps[:])
+        nc.vector.tensor_copy(out=haT[:], in_=haT_ps[:])
         for c in range(2):
             for i in range(NT):
                 cs = slice(c * HALF, (c + 1) * HALF)
                 ps = psum.tile([P, HALF], F32, name="lora_ps", tag="bank")
                 nc.tensor.matmul(out=ps[:], lhsT=haT[:, i, :], rhs=b_sb[:, cs], start=True, stop=True)
-                nc.scalar.copy(out=lora[i][:, cs], in_=ps[:])
+                evacuate("V" if i % 2 == 0 else "S", lora[i][:, cs], ps[:])
 
         wg4 = {}
         wc = {}
@@ -125,25 +131,25 @@ def tile_loramlp_pb_kernel(tc, h, ha, W_down, B_down, out):
         hc = [keep.tile([P, 512], U32, name="hc%d" % i, align_bytes=64) for i in range(NT + 1)]
         hs = [keep.tile([P, 512], U8, name="hs%d" % i, align_bytes=64) for i in range(NT + 1)]
 
-        def h_bank(which, b, blocks, eng):
+        def h_bank(which, b, blocks):
             dst = hg[which][:].bitcast(F32).rearrange("p (b r u) -> p b r u", b=4, r=P, u=2)
             xt = psum.tile([P, 2, 2, P], F32, name="xt", tag="bank")
             for n, (i, g) in enumerate(blocks):
                 words = h_raw[i][:].bitcast(F32)
                 for u in range(2):
                     nc.tensor.transpose(xt[:, n, u, :], words[:, 256 * g + u : 256 * (g + 1) : 2], ident_f[:])
-            evacuate(eng, dst[:, b : b + 2], xt[:].rearrange("p b u r -> p b r u"))
+            nc.scalar.copy(out=dst[:, b : b + 2], in_=xt[:].rearrange("p b u r -> p b r u"))
 
         def h_quant(which):
             nc.vector.quantize_mx(out=hc[which][:].bitcast(FP8X4), scales=hs[which][:], in_=hg[which][:])
 
         for i in (0, 2):
-            h_bank(i, 0, [(i, 0), (i, 1)], "V")
-            h_bank(i, 2, [(i, 2), (i, 3)], "S")
-            h_bank(i + 1, 0, [(i + 1, 0), (i + 1, 1)], "V")
+            h_bank(i, 0, [(i, 0), (i, 1)])
+            h_bank(i, 2, [(i, 2), (i, 3)])
+            h_bank(i + 1, 0, [(i + 1, 0), (i + 1, 1)])
             h_quant(i)
-            h_bank(i + 1, 2, [(i + 1, 2), (i + 1, 3)], "S")
-            h_bank(NT, i, [(i, LAST), (i + 1, LAST)], "S")
+            h_bank(i + 1, 2, [(i + 1, 2), (i + 1, 3)])
+            h_bank(NT, i, [(i, LAST), (i + 1, LAST)])
             h_quant(i + 1)
         h_quant(NT)
 
@@ -165,14 +171,9 @@ def tile_loramlp_pb_kernel(tc, h, ha, W_down, B_down, out):
                     stop=(g == LAST),
                 )
 
-        def finish(i, c, by_gpsimd=False):
+        def finish(i, c):
             cs = slice(c * HALF, (c + 1) * HALF)
-            if by_gpsimd:
-                sums = keep.tile([P, HALF], F32, name="sums%d%d" % (i, c))
-                nc.scalar.copy(out=sums[:], in_=acc[(i, c)][:])
-                nc.gpsimd.tensor_tensor(out=lora[i][:, cs], in0=sums[:], in1=lora[i][:, cs], op=ADD)
-            else:
-                nc.vector.tensor_tensor(out=lora[i][:, cs], in0=acc[(i, c)][:], in1=lora[i][:, cs], op=ADD)
+            nc.vector.tensor_tensor(out=lora[i][:, cs], in0=acc[(i, c)][:], in1=lora[i][:, cs], op=ADD)
             nc.sync.dma_start(out=out_v[:, i, cs], in_=lora[i][:, cs])
 
         mx_passes(0, 0)
@@ -184,7 +185,7 @@ def tile_loramlp_pb_kernel(tc, h, ha, W_down, B_down, out):
                 mx_passes(*HALVES[n - 1])
             if (g, c) == (3, 1):
                 finish(0, 0)
-                finish(1, 0, by_gpsimd=True)
+                finish(1, 0)
         finish(2, 0)
         w_quant(LAST, 1)
         mx_passes(LAST, 1)

@@ -27,8 +27,6 @@ HALVES = [(1, 0), (1, 1), (2, 0), (3, 0), (4, 0), (2, 1), (3, 1), (4, 1)]
 def vector_columns(g, c):
     if g == 0:
         return HALF
-    if (g, c) == (LAST, 0):
-        return 384
     return 128 if g > 1 and c == 1 else 256
 
 
@@ -71,9 +69,8 @@ def tile_loramlp_pb_kernel(tc, h, ha, W_down, B_down, out):
             h_raw.append(keep.tile([P, F], BF16, name="h_raw%d" % i))
             nc.sync.dma_start(out=h_raw[i][:], in_=h_v[:, i, :])
         load_chunk(1)
-        load_chunk(2)
         for c in range(2):
-            for g in (3, 4):
+            for g in (2, 3, 4):
                 load_half(g, c)
 
         ident_b = keep.tile([P, P], BF16, name="ident_b")
@@ -87,11 +84,22 @@ def tile_loramlp_pb_kernel(tc, h, ha, W_down, B_down, out):
             else:
                 nc.vector.tensor_copy(out=dst, in_=src)
 
+        zeros = keep.tile([P, 256], BF16, name="zeros")
+        nc.vector.memset(zeros[:], 0.0)
+        warm = psum.tile([P, 256], F32, name="warm", tag="bank")
+
+        def throwaway(n):
+            for k in range(n):
+                nc.tensor.matmul(out=warm[:], lhsT=zeros[:, :P], rhs=zeros[:], start=True, stop=True)
+
+        throwaway(6)
+
         lora = [keep.tile([P, D], F32, name="lora%d" % i) for i in range(NT)]
         haT = keep.tile([P, NT, P], BF16, name="haT")
         haT_ps = psum.tile([P, NT, P], BF16, name="haT_ps", tag="bank")
         for i in range(NT):
             nc.tensor.transpose(haT_ps[:, i, :], ha_sb[:, i, :], ident_b[:])
+        throwaway(2)
         nc.vector.tensor_copy(out=haT[:], in_=haT_ps[:])
         for c in range(2):
             for i in range(NT):

from contextlib import ExitStack

import concourse.mybir as mybir
from concourse.masks import make_identity

F32 = mybir.dt.float32
BF16 = mybir.dt.bfloat16
U32 = mybir.dt.uint32
U8 = mybir.dt.uint8
FP8X4 = mybir.dt.float8_e4m3fn_x4
ADD = mybir.AluOpType.add

P = 128
T, D, F, R = 512, 1024, 2560, 128
K_PASS = 512
G = F // K_PASS
NT = T // P
HALF = 512
LAST = G - 1

FLOPS = 2 * T * F * D + 2 * T * R * D


HALVES = [(1, 0), (1, 1), (2, 0), (3, 0), (4, 0), (2, 1), (3, 1), (4, 1)]


def vector_columns(g, c):
    if g == 0:
        return HALF
    return 128 if g > 1 and c == 1 else 256


def tile_loramlp_pb_kernel(tc, h, ha, W_down, B_down, out):
    nc = tc.nc
    with ExitStack() as ctx:
        keep = ctx.enter_context(tc.tile_pool(name="keep", bufs=1))
        psum = ctx.enter_context(tc.psum_pool(name="psum", bufs=8))
        ctx.enter_context(tc.manual_schedule())

        h_v = h.rearrange("(p i) k -> p i k", i=NT)
        out_v = out.rearrange("(p i) d -> p i d", i=NT)

        ha_sb = keep.tile([P, NT, R], BF16, name="ha_sb")
        b_sb = keep.tile([P, D], BF16, name="b_sb")
        nc.sync.dma_start(out=ha_sb[:], in_=ha.rearrange("(p i) r -> p i r", i=NT))
        nc.sync.dma_start(out=b_sb[:], in_=B_down)
        w_half = {}

        def load_half(g, c):
            wh = keep.tile([P, 4, HALF], BF16, name="w_raw%d%d" % (g, c))
            nc.sync.dma_start(
                out=wh[:],
                in_=W_down[g * K_PASS : (g + 1) * K_PASS, c * HALF : (c + 1) * HALF].rearrange("(p t) c -> p t c", t=4),
            )
            w_half[(g, c)] = wh[:]

        def load_chunk(g):
            wg = keep.tile([P, 4, D], BF16, name="w_raw%d" % g)
            nc.sync.dma_start(
                out=wg[:].rearrange("p t c -> p (t c)"),
                in_=W_down[g * K_PASS : (g + 1) * K_PASS, :].rearrange("(p t) c -> p (t c)", t=4),
            )
            for c in range(2):
                w_half[(g, c)] = wg[:, :, c * HALF : (c + 1) * HALF]

        h_raw = []
        load_chunk(0)
        for i in range(NT):
            h_raw.append(keep.tile([P, F], BF16, name="h_raw%d" % i))
            nc.sync.dma_start(out=h_raw[i][:], in_=h_v[:, i, :])
        load_chunk(1)
        for c in range(2):
            for g in (2, 3, 4):
                load_half(g, c)

        ident_b = keep.tile([P, P], BF16, name="ident_b")
        make_identity(nc, ident_b[:])
        ident_f = keep.tile([P, P], F32, name="ident_f")
        make_identity(nc, ident_f[:])

        def evacuate(eng, dst, src):
            if eng == "S":
                nc.scalar.copy(out=dst, in_=src)
            else:
                nc.vector.tensor_copy(out=dst, in_=src)

        zeros = keep.tile([P, 256], BF16, name="zeros")
        nc.vector.memset(zeros[:], 0.0)
        warm = psum.tile([P, 256], F32, name="warm", tag="bank")

        def throwaway(n):
            for k in range(n):
                nc.tensor.matmul(out=warm[:], lhsT=zeros[:, :P], rhs=zeros[:], start=True, stop=True)

        throwaway(6)

        lora = [keep.tile([P, D], F32, name="lora%d" % i) for i in range(NT)]
        haT = keep.tile([P, NT, P], BF16, name="haT")
        haT_ps = psum.tile([P, NT, P], BF16, name="haT_ps", tag="bank")
        for i in range(NT):
            nc.tensor.transpose(haT_ps[:, i, :], ha_sb[:, i, :], ident_b[:])
        throwaway(2)
        nc.vector.tensor_copy(out=haT[:], in_=haT_ps[:])
        for c in range(2):
            for i in range(NT):
                cs = slice(c * HALF, (c + 1) * HALF)
                ps = psum.tile([P, HALF], F32, name="lora_ps", tag="bank")
                nc.tensor.matmul(out=ps[:], lhsT=haT[:, i, :], rhs=b_sb[:, cs], start=True, stop=True)
                evacuate("V" if i % 2 == 0 else "S", lora[i][:, cs], ps[:])

        wg4 = {}
        wc = {}
        ws = {}

        def w_regroup(g, c):
            wg4[(g, c)] = keep.tile([P, HALF, 4], BF16, name="wg%d%d" % (g, c), align_bytes=64)
            a = vector_columns(g, c)
            for eng, lo, hi in (("S", a, HALF), ("V", 0, a)):
                if lo < hi:
                    evacuate(
                        eng,
                        wg4[(g, c)][:, lo:hi, :].rearrange("p (c i) t -> p c t i", i=4),
                        w_half[(g, c)][:, :, lo:hi].rearrange("p t (c i) -> p c t i", i=4),
                    )

        def w_quant(g, c):
            wc[(g, c)] = keep.tile([P, HALF], U32, name="wc%d%d" % (g, c), align_bytes=64)
            ws[(g, c)] = keep.tile([P, HALF], U8, name="ws%d%d" % (g, c), align_bytes=64)
            nc.vector.quantize_mx(
                out=wc[(g, c)][:].bitcast(FP8X4), scales=ws[(g, c)][:], in_=wg4[(g, c)][:].rearrange("p c t -> p (c t)")
            )

        for c in range(2):
            w_regroup(0, c)
        for c in range(2):
            w_quant(0, c)

        hg = [keep.tile([P, 2048], BF16, name="hg%d" % i, align_bytes=64) for i in range(NT + 1)]
        hc = [keep.tile([P, 512], U32, name="hc%d" % i, align_bytes=64) for i in range(NT + 1)]
        hs = [keep.tile([P, 512], U8, name="hs%d" % i, align_bytes=64) for i in range(NT + 1)]

        def h_bank(which, b, blocks):
            dst = hg[which][:].bitcast(F32).rearrange("p (b r u) -> p b r u", b=4, r=P, u=2)
            xt = psum.tile([P, 2, 2, P], F32, name="xt", tag="bank")
            for n, (i, g) in enumerate(blocks):
                words = h_raw[i][:].bitcast(F32)
                for u in range(2):
                    nc.tensor.transpose(xt[:, n, u, :], words[:, 256 * g + u : 256 * (g + 1) : 2], ident_f[:])
            nc.scalar.copy(out=dst[:, b : b + 2], in_=xt[:].rearrange("p b u r -> p b r u"))

        def h_quant(which):
            nc.vector.quantize_mx(out=hc[which][:].bitcast(FP8X4), scales=hs[which][:], in_=hg[which][:])

        for i in (0, 2):
            h_bank(i, 0, [(i, 0), (i, 1)])
            h_bank(i, 2, [(i, 2), (i, 3)])
            h_bank(i + 1, 0, [(i + 1, 0), (i + 1, 1)])
            h_quant(i)
            h_bank(i + 1, 2, [(i + 1, 2), (i + 1, 3)])
            h_bank(NT, i, [(i, LAST), (i + 1, LAST)])
            h_quant(i + 1)
        h_quant(NT)

        acc = {}

        def mx_passes(g, c):
            for i in range(NT):
                if g == 0:
                    acc[(i, c)] = psum.tile([P, HALF], F32, name="acc%d%d" % (i, c), tag="bank")
                which, block = (i, g) if g < LAST else (NT, i)
                hw = slice(block * P, (block + 1) * P)
                nc.tensor.matmul_mx(
                    out=acc[(i, c)][:],
                    lhsT=hc[which][:, hw].bitcast(FP8X4),
                    lhsT_scale=hs[which][:, hw],
                    rhs=wc[(g, c)][:].bitcast(FP8X4),
                    rhs_scale=ws[(g, c)][:],
                    start=(g == 0),
                    stop=(g == LAST),
                )

        def finish(i, c):
            cs = slice(c * HALF, (c + 1) * HALF)
            nc.vector.tensor_tensor(out=lora[i][:, cs], in0=acc[(i, c)][:], in1=lora[i][:, cs], op=ADD)
            nc.sync.dma_start(out=out_v[:, i, cs], in_=lora[i][:, cs])

        mx_passes(0, 0)
        mx_passes(0, 1)
        for n, (g, c) in enumerate(HALVES):
            w_regroup(g, c)
            if n > 0:
                w_quant(*HALVES[n - 1])
                mx_passes(*HALVES[n - 1])
            if (g, c) == (3, 1):
                finish(0, 0)
                finish(1, 0)
        finish(2, 0)
        w_quant(LAST, 1)
        mx_passes(LAST, 1)
        finish(3, 0)
        for i in range(NT):
            finish(i, 1)
